import numpy as np
import ml_dtypes


def mxq(x, axis, fmt="e4m3"):
    dtype, down = {"e4m3": (ml_dtypes.float8_e4m3fn, 7), "e5m2": (ml_dtypes.float8_e5m2, 14)}[fmt]
    v = np.moveaxis(np.asarray(x, np.float32).astype(ml_dtypes.bfloat16).astype(np.float64), axis, -1)
    blocks = v.reshape(v.shape[:-1] + (-1, 32))
    amax = np.abs(blocks).max(-1, keepdims=True)
    byte = np.maximum(np.where(amax > 0, np.frexp(amax)[1] - 1 + 127, 0) - down, 1)
    scale = np.exp2(byte - 127.0)
    codes = (blocks / scale).astype(np.float32).astype(dtype).astype(np.float64)
    return np.moveaxis((codes * scale).reshape(v.shape), -1, axis)


BF16 = ml_dtypes.bfloat16


def bf(x):
    return np.asarray(x, np.float32).astype(BF16)


def f64(x):
    return np.asarray(x).astype(np.float64)


B, C, H, W, R = 8, 512, 32, 16, 4
N = H * W
NOISE = 0.5


def mix(a, z):
    return sum(a[:, :, r, None] * z[:, r, None, :] for r in range(R))


def softmax(s):
    e = np.exp(s - s.max(-1, keepdims=True))
    return e / e.sum(-1, keepdims=True)


def setup_inputs():
    z = np.random.standard_normal((B, R, N))
    a1 = np.random.standard_normal((B, C, R)) / np.sqrt(R)
    a2 = np.random.standard_normal((B, C, R)) / np.sqrt(R)
    x1 = mix(a1, z) + NOISE * np.random.standard_normal((B, C, N))
    x2 = mix(a2, z) + NOISE * np.random.standard_normal((B, C, N))
    u1 = a1 / np.sqrt((a1 * a1).sum(2, keepdims=True) + NOISE * NOISE)
    u2 = a2 / np.sqrt((a2 * a2).sum(2, keepdims=True) + NOISE * NOISE)
    logits1 = mix(u1 + u2, u1.transpose(0, 2, 1))
    logits2 = mix(u2 + u1, u2.transpose(0, 2, 1))
    return {"logits1": bf(logits1), "logits2": bf(logits2),
            "x1": bf(x1.reshape(B, C, H, W)), "x2": bf(x2.reshape(B, C, H, W))}


def reference(logits1, logits2, x1, x2):
    x1f = f64(x1)
    x2f = f64(x2)
    x111 = x1f.reshape(B, C, N)
    x211 = x2f.reshape(B, C, N)
    attn11 = softmax(f64(logits1))
    attn22 = softmax(f64(logits2))
    y1 = mxq(attn11, 2, "e4m3") @ mxq(x111, 1, "e4m3")
    y2 = mxq(attn22, 2, "e4m3") @ mxq(x211, 1, "e4m3")
    x1_o = y1.transpose(0, 2, 1).reshape(B, C, H, W) + x1f
    x2_o = y2.transpose(0, 2, 1).reshape(B, C, H, W) + x2f
    return x1_o + x2_o

@@ -1,0 +1,185 @@
+from contextlib import ExitStack
+
+import concourse.mybir as mybir
+from concourse.masks import make_identity
+
+F32 = mybir.dt.float32
+BF16 = mybir.dt.bfloat16
+U32 = mybir.dt.uint32
+U8 = mybir.dt.uint8
+FP8X4 = mybir.dt.float8_e4m3fn_x4
+ALU = mybir.AluOpType
+ACT = mybir.ActivationFunctionType
+
+P = 128
+PACK = 4
+B = 8
+C = 512
+N = 512
+ROW_TILES = C // P
+UNITS = 2 * B
+AHEAD = 4
+X_BLOCKS_ON_VECTOR = 2
+
+FLOPS = 2 * 2 * B * C * C * N
+
+
+def tile_interfusion_pb_t_kernel(tc, logits1, logits2, x1, x2, out):
+    nc = tc.nc
+    logits = (logits1, logits2)
+    xs = (x1, x2)
+
+    with ExitStack() as ctx:
+        const = ctx.enter_context(tc.tile_pool(name="const", bufs=1))
+        lg_pool = ctx.enter_context(tc.tile_pool(name="lg_pool", bufs=6))
+        x_pool = ctx.enter_context(tc.tile_pool(name="x_pool", bufs=6))
+        stat = ctx.enter_context(tc.tile_pool(name="stat", bufs=4))
+        work = ctx.enter_context(tc.tile_pool(name="work", bufs=2))
+        mx_pool = ctx.enter_context(tc.tile_pool(name="mx_pool", bufs=6))
+        flip_psum = ctx.enter_context(tc.psum_pool(name="flip_psum", bufs=4))
+        acc_psum = ctx.enter_context(tc.psum_pool(name="acc_psum", bufs=4))
+
+        ident = const.tile([P, P], F32)
+        make_identity(nc, ident[:])
+
+        lg, xin, negmax, expd, rowsum, prob, flipped = {}, {}, {}, {}, {}, {}, {}
+        p_grouped, p_codes, p_scales = {}, {}, {}
+        x_grouped, x_codes, x_scales = {}, {}, {}
+        resid, acc = {}, {}
+
+        def load(u):
+            b, s = divmod(u, 2)
+            lg[u] = lg_pool.tile([P, ROW_TILES, C], BF16, name="lg", tag="lg")
+            nc.sync.dma_start(out=lg[u][:], in_=logits[s][b].rearrange("(j p) k -> p j k", p=P))
+            xin[u] = x_pool.tile([P, PACK, N], BF16, name="xin", tag="xin")
+            nc.sync.dma_start(out=xin[u][:], in_=xs[s][b].rearrange("(q t) h w -> q t (h w)", t=PACK))
+
+        def row_max(u):
+            unused = work.tile([P, ROW_TILES, C], BF16, name="unused", tag="unused")
+            negmax[u] = stat.tile([P, ROW_TILES], F32, name="negmax", tag="negmax")
+            for j in range(ROW_TILES):
+                nc.vector.tensor_scalar(
+                    out=unused[:, j, :],
+                    in0=lg[u][:, j, :],
+                    scalar1=-1.0,
+                    scalar2=None,
+                    op0=ALU.mult,
+                    op1=ALU.min,
+                    accum_out=negmax[u][:, j : j + 1],
+                )
+
+        def exponent(u):
+            expd[u] = work.tile([P, ROW_TILES, C], F32, name="expd", tag="expd")
+            rowsum[u] = stat.tile([P, ROW_TILES], F32, name="rowsum", tag="rowsum")
+            for j in range(ROW_TILES):
+                nc.scalar.activation(
+                    out=expd[u][:, j, :],
+                    in_=lg[u][:, j, :],
+                    func=ACT.Exp,
+                    bias=negmax[u][:, j : j + 1],
+                    scale=1.0,
+                    accum_out=rowsum[u][:, j : j + 1],
+                )
+
+        def normalise(u):
+            inv = stat.tile([P, ROW_TILES], F32, name="inv", tag="inv")
+            nc.vector.reciprocal(out=inv[:], in_=rowsum[u][:])
+            prob[u] = work.tile([P, ROW_TILES, C], BF16, name="prob", tag="prob")
+            for j in range(ROW_TILES):
+                nc.vector.tensor_scalar_mul(out=prob[u][:, j, :], in0=expd[u][:, j, :], scalar1=inv[:, j : j + 1])
+
+        def flip(u):
+            words = prob[u][:].bitcast(F32).rearrange("c j (q half) -> c j half q", half=2)
+            flipped[u] = []
+            for pair in range(ROW_TILES // 2):
+                bank = flip_psum.tile([P, 2, 2 * P], F32, name="bank", tag="bank")
+                for jj in range(2):
+                    for half in range(2):
+                        nc.tensor.transpose(
+                            bank[:, half, jj * P : (jj + 1) * P], words[:, 2 * pair + jj, half, :], ident[:]
+                        )
+                flipped[u].append(bank)
+
+        def group_p(u):
+            p_grouped[u] = work.tile([P, C, PACK], BF16, name="p_grouped", tag="p_grouped", align_bytes=64)
+            as_words = p_grouped[u][:].bitcast(F32)
+            for pair in range(ROW_TILES // 2):
+                nc.scalar.copy(
+                    out=as_words[:, 2 * pair * P : 2 * (pair + 1) * P, :],
+                    in_=flipped[u][pair][:].rearrange("q half c -> q c half"),
+                )
+
+        def quantise(grouped, codes, scales, u, label):
+            codes[u] = mx_pool.tile([P, C], U32, name=label + "_codes", tag=label + "_codes", align_bytes=64)
+            scales[u] = mx_pool.tile([P, C], U8, name=label + "_scales", tag=label + "_scales", align_bytes=64)
+            nc.vector.quantize_mx(
+                out=codes[u][:].bitcast(FP8X4),
+                scales=scales[u][:],
+                in_=grouped[u][:].rearrange("q c t -> q (c t)"),
+            )
+
+        def group_x(u):
+            x_grouped[u] = work.tile([P, N, PACK], BF16, name="x_grouped", tag="x_grouped", align_bytes=64)
+            dst = x_grouped[u][:].rearrange("q (j m) t -> q j m t", j=PACK)
+            src = xin[u][:].rearrange("q t (m j) -> q j m t", j=PACK)
+            cut = X_BLOCKS_ON_VECTOR
+            nc.vector.tensor_copy(out=dst[:, :cut], in_=src[:, :cut])
+            nc.scalar.copy(out=dst[:, cut:], in_=src[:, cut:])
+
+        def residual(b):
+            resid[b] = work.tile([P, PACK, C], F32, name="resid", tag="resid")
+            for j in range(PACK):
+                nc.gpsimd.tensor_tensor(
+                    out=resid[b][:, j, :], in0=xin[2 * b][:, j, :], in1=xin[2 * b + 1][:, j, :], op=ALU.add
+                )
+
+        def multiply(b):
+            acc[b] = []
+            for j in range(PACK):
+                bank = acc_psum.tile([P, C], F32, name="acc", tag="acc")
+                for s in range(2):
+                    u = 2 * b + s
+                    nc.tensor.matmul_mx(
+                        out=bank[:],
+                        lhsT=x_codes[u][:, j * P : (j + 1) * P].bitcast(FP8X4),
+                        lhsT_scale=x_scales[u][:, j * P : (j + 1) * P],
+                        rhs=p_codes[u][:].bitcast(FP8X4),
+                        rhs_scale=p_scales[u][:],
+                        start=(s == 0),
+                        stop=(s == 1),
+                    )
+                acc[b].append(bank)
+
+        def finish(b):
+            result = work.tile([P, PACK, C], F32, name="result", tag="result")
+            for j in range(PACK):
+                nc.vector.tensor_tensor(out=result[:, j, :], in0=acc[b][j][:], in1=resid[b][:, j, :], op=ALU.add)
+            nc.sync.dma_start(
+                out=out[b].rearrange("(m j) h w -> m (j h w)", j=PACK), in_=result[:].rearrange("m j c -> m (j c)")
+            )
+
+        def unit_stage(stage, u):
+            if 0 <= u < UNITS:
+                stage(u)
+
+        def batch_stage(stage, u):
+            if 0 <= u < UNITS and u % 2 == 1:
+                stage(u // 2)
+
+        for u in range(AHEAD):
+            load(u)
+        for step in range(UNITS + 6):
+            unit_stage(load, step + AHEAD)
+            unit_stage(row_max, step)
+            unit_stage(group_p, step - 3)
+            unit_stage(exponent, step - 1)
+            batch_stage(finish, step - 5)
+            unit_stage(normalise, step - 2)
+            unit_stage(flip, step - 2)
+            unit_stage(group_x, step - 1)
+            batch_stage(residual, step - 1)
+            if 0 <= step - 3 < UNITS:
+                quantise(p_grouped, p_codes, p_scales, step - 3, "p")
+            if 0 <= step - 2 < UNITS:
+                quantise(x_grouped, x_codes, x_scales, step - 2, "x")
+            batch_stage(multiply, step - 3)

@@ -129,7 +129,7 @@ def tile_interfusion_pb_t_kernel(tc, logits1, logits2, x1, x2, out):
         def residual(b):
             resid[b] = work.tile([P, PACK, C], F32, name="resid", tag="resid")
             for j in range(PACK):
-                nc.gpsimd.tensor_tensor(
+                nc.vector.tensor_tensor(
                     out=resid[b][:, j, :], in0=xin[2 * b][:, j, :], in1=xin[2 * b + 1][:, j, :], op=ALU.add
                 )
 

@@ -19,7 +19,7 @@ N = 512
 ROW_TILES = C // P
 UNITS = 2 * B
 AHEAD = 4
-X_BLOCKS_ON_VECTOR = 2
+X_BLOCKS_ON_VECTOR = 4
 
 FLOPS = 2 * 2 * B * C * C * N
 
@@ -124,12 +124,13 @@ def tile_interfusion_pb_t_kernel(tc, logits1, logits2, x1, x2, out):
             src = xin[u][:].rearrange("q t (m j) -> q j m t", j=PACK)
             cut = X_BLOCKS_ON_VECTOR
             nc.vector.tensor_copy(out=dst[:, :cut], in_=src[:, :cut])
-            nc.scalar.copy(out=dst[:, cut:], in_=src[:, cut:])
+            if cut < PACK:
+                nc.scalar.copy(out=dst[:, cut:], in_=src[:, cut:])
 
         def residual(b):
             resid[b] = work.tile([P, PACK, C], F32, name="resid", tag="resid")
             for j in range(PACK):
-                nc.vector.tensor_tensor(
+                nc.gpsimd.tensor_tensor(
                     out=resid[b][:, j, :], in0=xin[2 * b][:, j, :], in1=xin[2 * b + 1][:, j, :], op=ALU.add
                 )
 

@@ -14,14 +14,13 @@ ACT = mybir.ActivationFunctionType
 P = 128
 PACK = 4
 B = 8
+STREAMS = 2
 C = 512
 N = 512
 ROW_TILES = C // P
-UNITS = 2 * B
-AHEAD = 4
-X_BLOCKS_ON_VECTOR = 4
+X_BLOCKS_ON_VECTOR = 1
 
-FLOPS = 2 * 2 * B * C * C * N
+FLOPS = 2 * STREAMS * B * C * C * N
 
 
 def tile_interfusion_pb_t_kernel(tc, logits1, logits2, x1, x2, out):
@@ -31,13 +30,14 @@ def tile_interfusion_pb_t_kernel(tc, logits1, logits2, x1, x2, out):
 
     with ExitStack() as ctx:
         const = ctx.enter_context(tc.tile_pool(name="const", bufs=1))
-        lg_pool = ctx.enter_context(tc.tile_pool(name="lg_pool", bufs=6))
-        x_pool = ctx.enter_context(tc.tile_pool(name="x_pool", bufs=6))
-        stat = ctx.enter_context(tc.tile_pool(name="stat", bufs=4))
-        work = ctx.enter_context(tc.tile_pool(name="work", bufs=2))
-        mx_pool = ctx.enter_context(tc.tile_pool(name="mx_pool", bufs=6))
+        in_pool = ctx.enter_context(tc.tile_pool(name="in_pool", bufs=4 * STREAMS))
+        stat = ctx.enter_context(tc.tile_pool(name="stat", bufs=3 * STREAMS))
+        work = ctx.enter_context(tc.tile_pool(name="work", bufs=2 * STREAMS))
+        short = ctx.enter_context(tc.tile_pool(name="short", bufs=STREAMS))
+        single = ctx.enter_context(tc.tile_pool(name="single", bufs=1))
         flip_psum = ctx.enter_context(tc.psum_pool(name="flip_psum", bufs=4))
         acc_psum = ctx.enter_context(tc.psum_pool(name="acc_psum", bufs=4))
+        ctx.enter_context(tc.manual_schedule())
 
         ident = const.tile([P, P], F32)
         make_identity(nc, ident[:])
@@ -47,140 +47,148 @@ def tile_interfusion_pb_t_kernel(tc, logits1, logits2, x1, x2, out):
         x_grouped, x_codes, x_scales = {}, {}, {}
         resid, acc = {}, {}
 
-        def load(u):
-            b, s = divmod(u, 2)
-            lg[u] = lg_pool.tile([P, ROW_TILES, C], BF16, name="lg", tag="lg")
-            nc.sync.dma_start(out=lg[u][:], in_=logits[s][b].rearrange("(j p) k -> p j k", p=P))
-            xin[u] = x_pool.tile([P, PACK, N], BF16, name="xin", tag="xin")
-            nc.sync.dma_start(out=xin[u][:], in_=xs[s][b].rearrange("(q t) h w -> q t (h w)", t=PACK))
+        def load_logits(b):
+            for s in range(STREAMS):
+                lg[b, s] = in_pool.tile([P, ROW_TILES, C], BF16, name="lg", tag="lg")
+                nc.sync.dma_start(out=lg[b, s][:], in_=logits[s][b].rearrange("(j p) k -> p j k", p=P))
 
-        def row_max(u):
-            unused = work.tile([P, ROW_TILES, C], BF16, name="unused", tag="unused")
-            negmax[u] = stat.tile([P, ROW_TILES], F32, name="negmax", tag="negmax")
-            for j in range(ROW_TILES):
-                nc.vector.tensor_scalar(
-                    out=unused[:, j, :],
-                    in0=lg[u][:, j, :],
-                    scalar1=-1.0,
-                    scalar2=None,
-                    op0=ALU.mult,
-                    op1=ALU.min,
-                    accum_out=negmax[u][:, j : j + 1],
-                )
+        def load_x(b):
+            for s in range(STREAMS):
+                xin[b, s] = in_pool.tile([P, PACK, N], BF16, name="xin", tag="xin")
+                nc.sync.dma_start(out=xin[b, s][:], in_=xs[s][b].rearrange("(q t) h w -> q t (h w)", t=PACK))
 
-        def exponent(u):
-            expd[u] = work.tile([P, ROW_TILES, C], F32, name="expd", tag="expd")
-            rowsum[u] = stat.tile([P, ROW_TILES], F32, name="rowsum", tag="rowsum")
-            for j in range(ROW_TILES):
-                nc.scalar.activation(
-                    out=expd[u][:, j, :],
-                    in_=lg[u][:, j, :],
-                    func=ACT.Exp,
-                    bias=negmax[u][:, j : j + 1],
-                    scale=1.0,
-                    accum_out=rowsum[u][:, j : j + 1],
-                )
+        def row_max(b):
+            for s in range(STREAMS):
+                unused = short.tile([P, ROW_TILES, C], BF16, name="unused", tag="unused")
+                negmax[b, s] = stat.tile([P, ROW_TILES], F32, name="negmax", tag="negmax")
+                for j in range(ROW_TILES):
+                    nc.vector.tensor_scalar(
+                        out=unused[:, j, :],
+                        in0=lg[b, s][:, j, :],
+                        scalar1=-1.0,
+                        scalar2=None,
+                        op0=ALU.mult,
+                        op1=ALU.min,
+                        accum_out=negmax[b, s][:, j : j + 1],
+                    )
 
-        def normalise(u):
-            inv = stat.tile([P, ROW_TILES], F32, name="inv", tag="inv")
-            nc.vector.reciprocal(out=inv[:], in_=rowsum[u][:])
-            prob[u] = work.tile([P, ROW_TILES, C], BF16, name="prob", tag="prob")
-            for j in range(ROW_TILES):
-                nc.vector.tensor_scalar_mul(out=prob[u][:, j, :], in0=expd[u][:, j, :], scalar1=inv[:, j : j + 1])
+        def exponent(b):
+            for s in range(STREAMS):
+                expd[b, s] = work.tile([P, ROW_TILES, C], F32, name="expd", tag="expd")
+                rowsum[b, s] = stat.tile([P, ROW_TILES], F32, name="rowsum", tag="rowsum")
+                for j in range(ROW_TILES):
+                    nc.scalar.activation(
+                        out=expd[b, s][:, j, :],
+                        in_=lg[b, s][:, j, :],
+                        func=ACT.Exp,
+                        bias=negmax[b, s][:, j : j + 1],
+                        scale=1.0,
+                        accum_out=rowsum[b, s][:, j : j + 1],
+                    )
 
-        def flip(u):
-            words = prob[u][:].bitcast(F32).rearrange("c j (q half) -> c j half q", half=2)
-            flipped[u] = []
-            for pair in range(ROW_TILES // 2):
-                bank = flip_psum.tile([P, 2, 2 * P], F32, name="bank", tag="bank")
-                for jj in range(2):
-                    for half in range(2):
-                        nc.tensor.transpose(
-                            bank[:, half, jj * P : (jj + 1) * P], words[:, 2 * pair + jj, half, :], ident[:]
-                        )
-                flipped[u].append(bank)
+        def normalise(b):
+            inv = {}
+            for s in range(STREAMS):
+                inv[s] = stat.tile([P, ROW_TILES], F32, name="inv", tag="inv")
+                nc.vector.reciprocal(out=inv[s][:], in_=rowsum[b, s][:])
+            for s in range(STREAMS):
+                prob[b, s] = work.tile([P, ROW_TILES, C], BF16, name="prob", tag="prob")
+                for j in range(ROW_TILES):
+                    nc.vector.tensor_scalar_mul(
+                        out=prob[b, s][:, j, :], in0=expd[b, s][:, j, :], scalar1=inv[s][:, j : j + 1]
+                    )
 
-        def group_p(u):
-            p_grouped[u] = work.tile([P, C, PACK], BF16, name="p_grouped", tag="p_grouped", align_bytes=64)
-            as_words = p_grouped[u][:].bitcast(F32)
-            for pair in range(ROW_TILES // 2):
-                nc.scalar.copy(
-                    out=as_words[:, 2 * pair * P : 2 * (pair + 1) * P, :],
-                    in_=flipped[u][pair][:].rearrange("q half c -> q c half"),
-                )
+        def flip(b):
+            for s in range(STREAMS):
+                words = prob[b, s][:].bitcast(F32).rearrange("c j (q half) -> c j half q", half=2)
+                flipped[b, s] = []
+                for pair in range(ROW_TILES // 2):
+                    bank = flip_psum.tile([P, 2, 2 * P], F32, name="bank", tag="bank")
+                    for jj in range(2):
+                        for half in range(2):
+                            nc.tensor.transpose(
+                                bank[:, half, jj * P : (jj + 1) * P], words[:, 2 * pair + jj, half, :], ident[:]
+                            )
+                    flipped[b, s].append(bank)
 
-        def quantise(grouped, codes, scales, u, label):
-            codes[u] = mx_pool.tile([P, C], U32, name=label + "_codes", tag=label + "_codes", align_bytes=64)
-            scales[u] = mx_pool.tile([P, C], U8, name=label + "_scales", tag=label + "_scales", align_bytes=64)
-            nc.vector.quantize_mx(
-                out=codes[u][:].bitcast(FP8X4),
-                scales=scales[u][:],
-                in_=grouped[u][:].rearrange("q c t -> q (c t)"),
-            )
+        def group_p(b):
+            for s in range(STREAMS):
+                p_grouped[b, s] = short.tile([P, C, PACK], BF16, name="p_grouped", tag="p_grouped", align_bytes=64)
+                as_words = p_grouped[b, s][:].bitcast(F32)
+                for pair in range(ROW_TILES // 2):
+                    nc.scalar.copy(
+                        out=as_words[:, 2 * pair * P : 2 * (pair + 1) * P, :],
+                        in_=flipped[b, s][pair][:].rearrange("q half c -> q c half"),
+                    )
 
-        def group_x(u):
-            x_grouped[u] = work.tile([P, N, PACK], BF16, name="x_grouped", tag="x_grouped", align_bytes=64)
-            dst = x_grouped[u][:].rearrange("q (j m) t -> q j m t", j=PACK)
-            src = xin[u][:].rearrange("q t (m j) -> q j m t", j=PACK)
+        def group_x(b):
             cut = X_BLOCKS_ON_VECTOR
-            nc.vector.tensor_copy(out=dst[:, :cut], in_=src[:, :cut])
-            if cut < PACK:
+            for s in range(STREAMS):
+                x_grouped[b, s] = work.tile([P, N, PACK], BF16, name="x_grouped", tag="x_grouped", align_bytes=64)
+                dst = x_grouped[b, s][:].rearrange("q (j m) t -> q j m t", j=PACK)
+                src = xin[b, s][:].rearrange("q t (m j) -> q j m t", j=PACK)
+                nc.vector.tensor_copy(out=dst[:, :cut], in_=src[:, :cut])
                 nc.scalar.copy(out=dst[:, cut:], in_=src[:, cut:])
 
+        def quantise(grouped, codes, scales, b, label):
+            for s in range(STREAMS):
+                codes[b, s] = work.tile([P, C], U32, name=label + "_codes", tag=label + "_codes", align_bytes=64)
+                scales[b, s] = work.tile([P, C], U8, name=label + "_scales", tag=label + "_scales", align_bytes=64)
+                nc.vector.quantize_mx(
+                    out=codes[b, s][:].bitcast(FP8X4),
+                    scales=scales[b, s][:],
+                    in_=grouped[b, s][:].rearrange("q c t -> q (c t)"),
+                )
+
+        def quantise_both(b):
+            quantise(x_grouped, x_codes, x_scales, b, "x")
+            quantise(p_grouped, p_codes, p_scales, b, "p")
+
         def residual(b):
-            resid[b] = work.tile([P, PACK, C], F32, name="resid", tag="resid")
+            resid[b] = single.tile([P, PACK, C], F32, name="resid", tag="resid")
             for j in range(PACK):
                 nc.gpsimd.tensor_tensor(
-                    out=resid[b][:, j, :], in0=xin[2 * b][:, j, :], in1=xin[2 * b + 1][:, j, :], op=ALU.add
+                    out=resid[b][:, j, :], in0=xin[b, 0][:, j, :], in1=xin[b, 1][:, j, :], op=ALU.add
                 )
 
         def multiply(b):
             acc[b] = []
             for j in range(PACK):
                 bank = acc_psum.tile([P, C], F32, name="acc", tag="acc")
-                for s in range(2):
-                    u = 2 * b + s
+                for s in range(STREAMS):
                     nc.tensor.matmul_mx(
                         out=bank[:],
-                        lhsT=x_codes[u][:, j * P : (j + 1) * P].bitcast(FP8X4),
-                        lhsT_scale=x_scales[u][:, j * P : (j + 1) * P],
-                        rhs=p_codes[u][:].bitcast(FP8X4),
-                        rhs_scale=p_scales[u][:],
+                        lhsT=x_codes[b, s][:, j * P : (j + 1) * P].bitcast(FP8X4),
+                        lhsT_scale=x_scales[b, s][:, j * P : (j + 1) * P],
+                        rhs=p_codes[b, s][:].bitcast(FP8X4),
+                        rhs_scale=p_scales[b, s][:],
                         start=(s == 0),
-                        stop=(s == 1),
+                        stop=(s == STREAMS - 1),
                     )
                 acc[b].append(bank)
 
         def finish(b):
-            result = work.tile([P, PACK, C], F32, name="result", tag="result")
+            result = short.tile([P, PACK, C], F32, name="result", tag="result")
+            rows = out[b].rearrange("(m j) h w -> m j (h w)", j=PACK)
             for j in range(PACK):
                 nc.vector.tensor_tensor(out=result[:, j, :], in0=acc[b][j][:], in1=resid[b][:, j, :], op=ALU.add)
-            nc.sync.dma_start(
-                out=out[b].rearrange("(m j) h w -> m (j h w)", j=PACK), in_=result[:].rearrange("m j c -> m (j c)")
-            )
+                if j % 2 == 1:
+                    nc.sync.dma_start(out=rows[:, j - 1 : j + 1, :], in_=result[:, j - 1 : j + 1, :])
 
-        def unit_stage(stage, u):
-            if 0 <= u < UNITS:
-                stage(u)
+        def stage(work_of, b):
+            if 0 <= b < B:
+                work_of(b)
 
-        def batch_stage(stage, u):
-            if 0 <= u < UNITS and u % 2 == 1:
-                stage(u // 2)
-
-        for u in range(AHEAD):
-            load(u)
-        for step in range(UNITS + 6):
-            unit_stage(load, step + AHEAD)
-            unit_stage(row_max, step)
-            unit_stage(group_p, step - 3)
-            unit_stage(exponent, step - 1)
-            batch_stage(finish, step - 5)
-            unit_stage(normalise, step - 2)
-            unit_stage(flip, step - 2)
-            unit_stage(group_x, step - 1)
-            batch_stage(residual, step - 1)
-            if 0 <= step - 3 < UNITS:
-                quantise(p_grouped, p_codes, p_scales, step - 3, "p")
-            if 0 <= step - 2 < UNITS:
-                quantise(x_grouped, x_codes, x_scales, step - 2, "x")
-            batch_stage(multiply, step - 3)
+        for i in range(-3, B + 2):
+            stage(load_logits, i + 3)
+            stage(load_x, i + 2)
+            stage(finish, i - 2)
+            stage(residual, i - 1)
+            stage(row_max, i + 2)
+            stage(group_p, i - 1)
+            stage(exponent, i + 1)
+            stage(quantise_both, i - 1)
+            stage(multiply, i - 1)
+            stage(normalise, i)
+            stage(flip, i)
+            stage(group_x, i)

@@ -18,7 +18,7 @@ STREAMS = 2
 C = 512
 N = 512
 ROW_TILES = C // P
-X_BLOCKS_ON_VECTOR = 1
+X_ROWS_ON_VECTOR = 32
 
 FLOPS = 2 * STREAMS * B * C * C * N
 
@@ -122,11 +122,11 @@ def tile_interfusion_pb_t_kernel(tc, logits1, logits2, x1, x2, out):
                     )
 
         def group_x(b):
-            cut = X_BLOCKS_ON_VECTOR
+            cut = X_ROWS_ON_VECTOR
             for s in range(STREAMS):
                 x_grouped[b, s] = work.tile([P, N, PACK], BF16, name="x_grouped", tag="x_grouped", align_bytes=64)
-                dst = x_grouped[b, s][:].rearrange("q (j m) t -> q j m t", j=PACK)
-                src = xin[b, s][:].rearrange("q t (m j) -> q j m t", j=PACK)
+                dst = x_grouped[b, s][:].rearrange("q (j m) t -> q m t j", j=PACK)
+                src = xin[b, s][:].rearrange("q t (m j) -> q m t j", j=PACK)
                 nc.vector.tensor_copy(out=dst[:, :cut], in_=src[:, :cut])
                 nc.scalar.copy(out=dst[:, cut:], in_=src[:, cut:])
 

@@ -18,7 +18,7 @@ STREAMS = 2
 C = 512
 N = 512
 ROW_TILES = C // P
-X_ROWS_ON_VECTOR = 32
+X_ROWS_FIRST, X_ROWS_STEADY, X_ROWS_LAST = 64, 24, 0
 
 FLOPS = 2 * STREAMS * B * C * C * N
 
@@ -57,20 +57,19 @@ def tile_interfusion_pb_t_kernel(tc, logits1, logits2, x1, x2, out):
                 xin[b, s] = in_pool.tile([P, PACK, N], BF16, name="xin", tag="xin")
                 nc.sync.dma_start(out=xin[b, s][:], in_=xs[s][b].rearrange("(q t) h w -> q t (h w)", t=PACK))
 
-        def row_max(b):
-            for s in range(STREAMS):
-                unused = short.tile([P, ROW_TILES, C], BF16, name="unused", tag="unused")
-                negmax[b, s] = stat.tile([P, ROW_TILES], F32, name="negmax", tag="negmax")
-                for j in range(ROW_TILES):
-                    nc.vector.tensor_scalar(
-                        out=unused[:, j, :],
-                        in0=lg[b, s][:, j, :],
-                        scalar1=-1.0,
-                        scalar2=None,
-                        op0=ALU.mult,
-                        op1=ALU.min,
-                        accum_out=negmax[b, s][:, j : j + 1],
-                    )
+        def row_max(b, s):
+            unused = short.tile([P, ROW_TILES, C], BF16, name="unused", tag="unused")
+            negmax[b, s] = stat.tile([P, ROW_TILES], F32, name="negmax", tag="negmax")
+            for j in range(ROW_TILES):
+                nc.vector.tensor_scalar(
+                    out=unused[:, j, :],
+                    in0=lg[b, s][:, j, :],
+                    scalar1=-1.0,
+                    scalar2=None,
+                    op0=ALU.mult,
+                    op1=ALU.min,
+                    accum_out=negmax[b, s][:, j : j + 1],
+                )
 
         def exponent(b):
             for s in range(STREAMS):
@@ -94,9 +93,11 @@ def tile_interfusion_pb_t_kernel(tc, logits1, logits2, x1, x2, out):
             for s in range(STREAMS):
                 prob[b, s] = work.tile([P, ROW_TILES, C], BF16, name="prob", tag="prob")
                 for j in range(ROW_TILES):
-                    nc.vector.tensor_scalar_mul(
-                        out=prob[b, s][:, j, :], in0=expd[b, s][:, j, :], scalar1=inv[s][:, j : j + 1]
-                    )
+                    p_row, exp_row, factor = prob[b, s][:, j, :], expd[b, s][:, j, :], inv[s][:, j : j + 1]
+                    if b == B - 1 and s == STREAMS - 1:
+                        nc.scalar.activation(out=p_row, in_=exp_row, func=ACT.Copy, scale=factor)
+                    else:
+                        nc.vector.tensor_scalar_mul(out=p_row, in0=exp_row, scalar1=factor)
 
         def flip(b):
             for s in range(STREAMS):
@@ -122,12 +123,13 @@ def tile_interfusion_pb_t_kernel(tc, logits1, logits2, x1, x2, out):
                     )
 
         def group_x(b):
-            cut = X_ROWS_ON_VECTOR
+            cut = X_ROWS_FIRST if b < 2 else X_ROWS_LAST if b == B - 1 else X_ROWS_STEADY
             for s in range(STREAMS):
                 x_grouped[b, s] = work.tile([P, N, PACK], BF16, name="x_grouped", tag="x_grouped", align_bytes=64)
                 dst = x_grouped[b, s][:].rearrange("q (j m) t -> q m t j", j=PACK)
                 src = xin[b, s][:].rearrange("q t (m j) -> q m t j", j=PACK)
-                nc.vector.tensor_copy(out=dst[:, :cut], in_=src[:, :cut])
+                if cut > 0:
+                    nc.vector.tensor_copy(out=dst[:, :cut], in_=src[:, :cut])
                 nc.scalar.copy(out=dst[:, cut:], in_=src[:, cut:])
 
         def quantise(grouped, codes, scales, b, label):
@@ -144,10 +146,11 @@ def tile_interfusion_pb_t_kernel(tc, logits1, logits2, x1, x2, out):
             quantise(x_grouped, x_codes, x_scales, b, "x")
             quantise(p_grouped, p_codes, p_scales, b, "p")
 
-        def residual(b):
-            resid[b] = single.tile([P, PACK, C], F32, name="resid", tag="resid")
-            for j in range(PACK):
-                nc.gpsimd.tensor_tensor(
+        def residual(b, engine, blocks):
+            if b not in resid:
+                resid[b] = single.tile([P, PACK, C], F32, name="resid", tag="resid")
+            for j in blocks:
+                engine.tensor_tensor(
                     out=resid[b][:, j, :], in0=xin[b, 0][:, j, :], in1=xin[b, 1][:, j, :], op=ALU.add
                 )
 
@@ -167,28 +170,40 @@ def tile_interfusion_pb_t_kernel(tc, logits1, logits2, x1, x2, out):
                     )
                 acc[b].append(bank)
 
-        def finish(b):
-            result = short.tile([P, PACK, C], F32, name="result", tag="result")
+        def finish(b, half):
+            result = work.tile([P, 2, C], F32, name="result", tag="result")
             rows = out[b].rearrange("(m j) h w -> m j (h w)", j=PACK)
-            for j in range(PACK):
-                nc.vector.tensor_tensor(out=result[:, j, :], in0=acc[b][j][:], in1=resid[b][:, j, :], op=ALU.add)
-                if j % 2 == 1:
-                    nc.sync.dma_start(out=rows[:, j - 1 : j + 1, :], in_=result[:, j - 1 : j + 1, :])
+            for jj in range(2):
+                j = 2 * half + jj
+                nc.vector.tensor_tensor(out=result[:, jj, :], in0=acc[b][j][:], in1=resid[b][:, j, :], op=ALU.add)
+            nc.sync.dma_start(out=rows[:, 2 * half : 2 * half + 2, :], in_=result[:])
 
-        def stage(work_of, b):
+        def stage(work_of, b, *more):
             if 0 <= b < B:
-                work_of(b)
+                work_of(b, *more)
 
-        for i in range(-3, B + 2):
-            stage(load_logits, i + 3)
+        for b in range(2):
+            load_logits(b)
+            load_x(b)
+        for i in range(B + 2):
+            stage(load_logits, i + 2)
             stage(load_x, i + 2)
-            stage(finish, i - 2)
-            stage(residual, i - 1)
-            stage(row_max, i + 2)
+            for half in range(2):
+                stage(finish, i - 2, half)
+                stage(row_max, i, half)
+            if 2 <= i < B:
+                residual(i - 1, nc.gpsimd, range(PACK))
+            elif i == B:
+                residual(B - 1, nc.gpsimd, range(2))
             stage(group_p, i - 1)
-            stage(exponent, i + 1)
+            if i == B:
+                residual(B - 1, nc.vector, range(2, PACK))
+            stage(exponent, i)
+            if i == 0:
+                residual(0, nc.vector, range(PACK))
+                group_x(0)
             stage(quantise_both, i - 1)
             stage(multiply, i - 1)
             stage(normalise, i)
             stage(flip, i)
-            stage(group_x, i)
+            stage(group_x, i + 1)

@@ -188,21 +188,20 @@ def tile_interfusion_pb_t_kernel(tc, logits1, logits2, x1, x2, out):
         for i in range(B + 2):
             stage(load_logits, i + 2)
             stage(load_x, i + 2)
-            for half in range(2):
-                stage(finish, i - 2, half)
-                stage(row_max, i, half)
-            if 2 <= i < B:
-                residual(i - 1, nc.gpsimd, range(PACK))
-            elif i == B:
-                residual(B - 1, nc.gpsimd, range(2))
+            stage(finish, i - 2, 0)
+            stage(finish, i - 2, 1)
+            if 2 <= i <= B:
+                residual(i - 1, nc.gpsimd, range(2, PACK))
+            stage(row_max, i, 0)
+            stage(row_max, i, 1)
             stage(group_p, i - 1)
-            if i == B:
-                residual(B - 1, nc.vector, range(2, PACK))
             stage(exponent, i)
             if i == 0:
                 residual(0, nc.vector, range(PACK))
                 group_x(0)
             stage(quantise_both, i - 1)
+            if 2 <= i <= B:
+                residual(i - 1, nc.vector, range(2))
             stage(multiply, i - 1)
             stage(normalise, i)
             stage(flip, i)

@@ -18,7 +18,8 @@ STREAMS = 2
 C = 512
 N = 512
 ROW_TILES = C // P
-X_ROWS_FIRST, X_ROWS_STEADY, X_ROWS_LAST = 64, 24, 0
+X_ROWS_ON_VECTOR = 40
+X_ROWS_ON_TENSOR = 48
 
 FLOPS = 2 * STREAMS * B * C * C * N
 
@@ -41,16 +42,21 @@ def tile_interfusion_pb_t_kernel(tc, logits1, logits2, x1, x2, out):
 
         ident = const.tile([P, P], F32)
         make_identity(nc, ident[:])
+        ident_bf16 = const.tile([P, P], BF16)
+        make_identity(nc, ident_bf16[:])
 
-        lg, xin, negmax, expd, rowsum, prob, flipped = {}, {}, {}, {}, {}, {}, {}
+        lg, xin, negmax, expd, rowsum, inv, prob, flipped = {}, {}, {}, {}, {}, {}, {}, {}
         p_grouped, p_codes, p_scales = {}, {}, {}
-        x_grouped, x_codes, x_scales = {}, {}, {}
+        spread, x_grouped, x_codes, x_scales = {}, {}, {}, {}
         resid, acc = {}, {}
 
         def load_logits(b):
             for s in range(STREAMS):
                 lg[b, s] = in_pool.tile([P, ROW_TILES, C], BF16, name="lg", tag="lg")
-                nc.sync.dma_start(out=lg[b, s][:], in_=logits[s][b].rearrange("(j p) k -> p j k", p=P))
+                rows = logits[s][b].rearrange("(j p) k -> p j k", p=P)
+                step = 1 if (b, s) == (0, 0) else ROW_TILES
+                for j in range(0, ROW_TILES, step):
+                    nc.sync.dma_start(out=lg[b, s][:, j : j + step, :], in_=rows[:, j : j + step, :])
 
         def load_x(b):
             for s in range(STREAMS):
@@ -85,15 +91,15 @@ def tile_interfusion_pb_t_kernel(tc, logits1, logits2, x1, x2, out):
                         accum_out=rowsum[b, s][:, j : j + 1],
                     )
 
+        def invert(b, s):
+            inv[b, s] = stat.tile([P, ROW_TILES], F32, name="inv", tag="inv")
+            nc.vector.reciprocal(out=inv[b, s][:], in_=rowsum[b, s][:])
+
         def normalise(b):
-            inv = {}
-            for s in range(STREAMS):
-                inv[s] = stat.tile([P, ROW_TILES], F32, name="inv", tag="inv")
-                nc.vector.reciprocal(out=inv[s][:], in_=rowsum[b, s][:])
             for s in range(STREAMS):
                 prob[b, s] = work.tile([P, ROW_TILES, C], BF16, name="prob", tag="prob")
                 for j in range(ROW_TILES):
-                    p_row, exp_row, factor = prob[b, s][:, j, :], expd[b, s][:, j, :], inv[s][:, j : j + 1]
+                    p_row, exp_row, factor = prob[b, s][:, j, :], expd[b, s][:, j, :], inv[b, s][:, j : j + 1]
                     if b == B - 1 and s == STREAMS - 1:
                         nc.scalar.activation(out=p_row, in_=exp_row, func=ACT.Copy, scale=factor)
                     else:
@@ -122,15 +128,34 @@ def tile_interfusion_pb_t_kernel(tc, logits1, logits2, x1, x2, out):
                         in_=flipped[b, s][pair][:].rearrange("q half c -> q c half"),
                     )
 
-        def group_x(b):
-            cut = X_ROWS_FIRST if b < 2 else X_ROWS_LAST if b == B - 1 else X_ROWS_STEADY
+        def spread_x(b):
+            for s in range(STREAMS):
+                spread[b, s] = flip_psum.tile([P, PACK, X_ROWS_ON_TENSOR, PACK], BF16, name="spread", tag="bank")
+                src = xin[b, s][:].rearrange("q t (m j) -> q j m t", j=PACK)[:, :, P - X_ROWS_ON_TENSOR :, :]
+                for j in range(0, PACK, 2):
+                    nc.tensor.matmul(
+                        spread[b, s][:, j : j + 2],
+                        lhsT=ident_bf16[:],
+                        rhs=src[:, j : j + 2],
+                        start=True,
+                        stop=True,
+                    )
+
+        def gather_x(b):
             for s in range(STREAMS):
                 x_grouped[b, s] = work.tile([P, N, PACK], BF16, name="x_grouped", tag="x_grouped", align_bytes=64)
+                blocks = x_grouped[b, s][:].rearrange("q (j m) t -> q j m t", j=PACK)
+                nc.scalar.copy(out=blocks[:, :, P - X_ROWS_ON_TENSOR :, :], in_=spread[b, s][:])
+
+        def group_x(b):
+            cut = X_ROWS_ON_VECTOR if b < 2 else 0
+            for s in range(STREAMS):
                 dst = x_grouped[b, s][:].rearrange("q (j m) t -> q m t j", j=PACK)
                 src = xin[b, s][:].rearrange("q t (m j) -> q m t j", j=PACK)
                 if cut > 0:
                     nc.vector.tensor_copy(out=dst[:, :cut], in_=src[:, :cut])
-                nc.scalar.copy(out=dst[:, cut:], in_=src[:, cut:])
+                end = P - X_ROWS_ON_TENSOR
+                nc.scalar.copy(out=dst[:, cut:end], in_=src[:, cut:end])
 
         def quantise(grouped, codes, scales, b, label):
             for s in range(STREAMS):
@@ -173,10 +198,12 @@ def tile_interfusion_pb_t_kernel(tc, logits1, logits2, x1, x2, out):
         def finish(b, half):
             result = work.tile([P, 2, C], F32, name="result", tag="result")
             rows = out[b].rearrange("(m j) h w -> m j (h w)", j=PACK)
+            step = 1 if b == B - 1 else 2
             for jj in range(2):
                 j = 2 * half + jj
                 nc.vector.tensor_tensor(out=result[:, jj, :], in0=acc[b][j][:], in1=resid[b][:, j, :], op=ALU.add)
-            nc.sync.dma_start(out=rows[:, 2 * half : 2 * half + 2, :], in_=result[:])
+                if jj % step == step - 1:
+                    nc.sync.dma_start(out=rows[:, j + 1 - step : j + 1, :], in_=result[:, jj + 1 - step : jj + 1, :])
 
         def stage(work_of, b, *more):
             if 0 <= b < B:
@@ -190,18 +217,24 @@ def tile_interfusion_pb_t_kernel(tc, logits1, logits2, x1, x2, out):
             stage(load_x, i + 2)
             stage(finish, i - 2, 0)
             stage(finish, i - 2, 1)
-            if 2 <= i <= B:
+            if 2 <= i < B:
                 residual(i - 1, nc.gpsimd, range(2, PACK))
             stage(row_max, i, 0)
             stage(row_max, i, 1)
             stage(group_p, i - 1)
             stage(exponent, i)
             if i == 0:
+                spread_x(0)
+                gather_x(0)
                 residual(0, nc.vector, range(PACK))
                 group_x(0)
+            stage(spread_x, i + 1)
             stage(quantise_both, i - 1)
+            stage(gather_x, i + 1)
+            stage(invert, i, 0)
             if 2 <= i <= B:
-                residual(i - 1, nc.vector, range(2))
+                residual(i - 1, nc.vector, range(2 if i < B else PACK))
+            stage(invert, i, 1)
             stage(multiply, i - 1)
             stage(normalise, i)
             stage(flip, i)

@@ -18,8 +18,10 @@ STREAMS = 2
 C = 512
 N = 512
 ROW_TILES = C // P
-X_ROWS_ON_VECTOR = 40
+X_ROWS_ON_VECTOR = 56
 X_ROWS_ON_TENSOR = 48
+GPSIMD_FIRST, GPSIMD_LAST = 1, B - 4
+LAST = (B - 1, STREAMS - 1)
 
 FLOPS = 2 * STREAMS * B * C * C * N
 
@@ -48,7 +50,7 @@ def tile_interfusion_pb_t_kernel(tc, logits1, logits2, x1, x2, out):
         lg, xin, negmax, expd, rowsum, inv, prob, flipped = {}, {}, {}, {}, {}, {}, {}, {}
         p_grouped, p_codes, p_scales = {}, {}, {}
         spread, x_grouped, x_codes, x_scales = {}, {}, {}, {}
-        resid, acc = {}, {}
+        resid, acc, result = {}, {}, {}
 
         def load_logits(b):
             for s in range(STREAMS):
@@ -95,28 +97,26 @@ def tile_interfusion_pb_t_kernel(tc, logits1, logits2, x1, x2, out):
             inv[b, s] = stat.tile([P, ROW_TILES], F32, name="inv", tag="inv")
             nc.vector.reciprocal(out=inv[b, s][:], in_=rowsum[b, s][:])
 
-        def normalise(b):
-            for s in range(STREAMS):
-                prob[b, s] = work.tile([P, ROW_TILES, C], BF16, name="prob", tag="prob")
-                for j in range(ROW_TILES):
-                    p_row, exp_row, factor = prob[b, s][:, j, :], expd[b, s][:, j, :], inv[b, s][:, j : j + 1]
-                    if b == B - 1 and s == STREAMS - 1:
-                        nc.scalar.activation(out=p_row, in_=exp_row, func=ACT.Copy, scale=factor)
-                    else:
-                        nc.vector.tensor_scalar_mul(out=p_row, in0=exp_row, scalar1=factor)
+        def normalise(b, s):
+            prob[b, s] = work.tile([P, ROW_TILES, C], BF16, name="prob", tag="prob")
+            for j in range(ROW_TILES):
+                p_row, exp_row, factor = prob[b, s][:, j, :], expd[b, s][:, j, :], inv[b, s][:, j : j + 1]
+                if (b, s) == LAST:
+                    nc.scalar.activation(out=p_row, in_=exp_row, func=ACT.Copy, scale=factor)
+                else:
+                    nc.vector.tensor_scalar_mul(out=p_row, in0=exp_row, scalar1=factor)
 
-        def flip(b):
-            for s in range(STREAMS):
-                words = prob[b, s][:].bitcast(F32).rearrange("c j (q half) -> c j half q", half=2)
-                flipped[b, s] = []
-                for pair in range(ROW_TILES // 2):
-                    bank = flip_psum.tile([P, 2, 2 * P], F32, name="bank", tag="bank")
-                    for jj in range(2):
-                        for half in range(2):
-                            nc.tensor.transpose(
-                                bank[:, half, jj * P : (jj + 1) * P], words[:, 2 * pair + jj, half, :], ident[:]
-                            )
-                    flipped[b, s].append(bank)
+        def flip(b, s):
+            words = prob[b, s][:].bitcast(F32).rearrange("c j (q half) -> c j half q", half=2)
+            flipped[b, s] = []
+            for pair in range(ROW_TILES // 2):
+                bank = flip_psum.tile([P, 2, 2 * P], F32, name="bank", tag="bank")
+                for jj in range(2):
+                    for half in range(2):
+                        nc.tensor.transpose(
+                            bank[:, half, jj * P : (jj + 1) * P], words[:, 2 * pair + jj, half, :], ident[:]
+                        )
+                flipped[b, s].append(bank)
 
         def group_p(b):
             for s in range(STREAMS):
@@ -130,7 +130,7 @@ def tile_interfusion_pb_t_kernel(tc, logits1, logits2, x1, x2, out):
 
         def spread_x(b):
             for s in range(STREAMS):
-                spread[b, s] = flip_psum.tile([P, PACK, X_ROWS_ON_TENSOR, PACK], BF16, name="spread", tag="bank")
+                spread[b, s] = acc_psum.tile([P, PACK, X_ROWS_ON_TENSOR, PACK], BF16, name="spread", tag="acc")
                 src = xin[b, s][:].rearrange("q t (m j) -> q j m t", j=PACK)[:, :, P - X_ROWS_ON_TENSOR :, :]
                 for j in range(0, PACK, 2):
                     nc.tensor.matmul(
@@ -157,27 +157,35 @@ def tile_interfusion_pb_t_kernel(tc, logits1, logits2, x1, x2, out):
                 end = P - X_ROWS_ON_TENSOR
                 nc.scalar.copy(out=dst[:, cut:end], in_=src[:, cut:end])
 
-        def quantise(grouped, codes, scales, b, label):
+        def quantise(grouped, codes, scales, label, b, s):
+            codes[b, s] = work.tile([P, C], U32, name=label + "_codes", tag=label + "_codes", align_bytes=64)
+            scales[b, s] = work.tile([P, C], U8, name=label + "_scales", tag=label + "_scales", align_bytes=64)
+            nc.vector.quantize_mx(
+                out=codes[b, s][:].bitcast(FP8X4),
+                scales=scales[b, s][:],
+                in_=grouped[b, s][:].rearrange("q c t -> q (c t)"),
+            )
+
+        def quantise_x(b):
             for s in range(STREAMS):
-                codes[b, s] = work.tile([P, C], U32, name=label + "_codes", tag=label + "_codes", align_bytes=64)
-                scales[b, s] = work.tile([P, C], U8, name=label + "_scales", tag=label + "_scales", align_bytes=64)
-                nc.vector.quantize_mx(
-                    out=codes[b, s][:].bitcast(FP8X4),
-                    scales=scales[b, s][:],
-                    in_=grouped[b, s][:].rearrange("q c t -> q (c t)"),
-                )
+                quantise(x_grouped, x_codes, x_scales, "x", b, s)
 
-        def quantise_both(b):
-            quantise(x_grouped, x_codes, x_scales, b, "x")
-            quantise(p_grouped, p_codes, p_scales, b, "p")
+        def quantise_p(b, s):
+            quantise(p_grouped, p_codes, p_scales, "p", b, s)
 
-        def residual(b, engine, blocks):
-            if b not in resid:
-                resid[b] = single.tile([P, PACK, C], F32, name="resid", tag="resid")
-            for j in blocks:
-                engine.tensor_tensor(
-                    out=resid[b][:, j, :], in0=xin[b, 0][:, j, :], in1=xin[b, 1][:, j, :], op=ALU.add
-                )
+        def add_rows(engine, b, first, last):
+            x_rows = [xin[b, s][:].rearrange("q t n -> q (t n)")[:, first:last] for s in range(STREAMS)]
+            sums = resid[b][:].rearrange("m j c -> m (j c)")[:, first:last]
+            engine.tensor_tensor(out=sums, in0=x_rows[0], in1=x_rows[1], op=ALU.add)
+
+        def residual(engine, b, blocks):
+            resid[b] = single.tile([P, PACK, C], F32, name="resid", tag="resid")
+            for j in range(blocks):
+                add_rows(engine, b, j * C, (j + 1) * C)
+
+        def residual_gpsimd(b):
+            add_rows(nc.gpsimd, b, 2 * C - 1, 3 * C)
+            add_rows(nc.gpsimd, b, 3 * C, 4 * C)
 
         def multiply(b):
             acc[b] = []
@@ -195,15 +203,16 @@ def tile_interfusion_pb_t_kernel(tc, logits1, logits2, x1, x2, out):
                     )
                 acc[b].append(bank)
 
-        def finish(b, half):
-            result = work.tile([P, 2, C], F32, name="result", tag="result")
+        def finish(b, j):
+            if j % 2 == 0:
+                result[b, j // 2] = work.tile([P, 2, C], F32, name="result", tag="result")
+            pair = result[b, j // 2]
+            nc.vector.tensor_tensor(out=pair[:, j % 2, :], in0=acc[b][j][:], in1=resid[b][:, j, :], op=ALU.add)
             rows = out[b].rearrange("(m j) h w -> m j (h w)", j=PACK)
-            step = 1 if b == B - 1 else 2
-            for jj in range(2):
-                j = 2 * half + jj
-                nc.vector.tensor_tensor(out=result[:, jj, :], in0=acc[b][j][:], in1=resid[b][:, j, :], op=ALU.add)
-                if jj % step == step - 1:
-                    nc.sync.dma_start(out=rows[:, j + 1 - step : j + 1, :], in_=result[:, jj + 1 - step : jj + 1, :])
+            if b == B - 1:
+                nc.sync.dma_start(out=rows[:, j : j + 1, :], in_=pair[:, j % 2 : j % 2 + 1, :])
+            elif j % 2 == 1:
+                nc.sync.dma_start(out=rows[:, j - 1 : j + 1, :], in_=pair[:])
 
         def stage(work_of, b, *more):
             if 0 <= b < B:
@@ -212,30 +221,56 @@ def tile_interfusion_pb_t_kernel(tc, logits1, logits2, x1, x2, out):
         for b in range(2):
             load_logits(b)
             load_x(b)
-        for i in range(B + 2):
+        for s in range(STREAMS):
+            row_max(0, s)
+        for i in range(B + 1):
+            if GPSIMD_FIRST <= i - 2 <= GPSIMD_LAST:
+                residual_gpsimd(i - 2)
             stage(load_logits, i + 2)
             stage(load_x, i + 2)
-            stage(finish, i - 2, 0)
-            stage(finish, i - 2, 1)
-            if 2 <= i < B:
-                residual(i - 1, nc.gpsimd, range(2, PACK))
-            stage(row_max, i, 0)
-            stage(row_max, i, 1)
-            stage(group_p, i - 1)
             stage(exponent, i)
             if i == 0:
                 spread_x(0)
+                residual(nc.vector, 0, PACK)
                 gather_x(0)
-                residual(0, nc.vector, range(PACK))
                 group_x(0)
-            stage(spread_x, i + 1)
-            stage(quantise_both, i - 1)
-            stage(gather_x, i + 1)
-            stage(invert, i, 0)
-            if 2 <= i <= B:
-                residual(i - 1, nc.vector, range(2 if i < B else PACK))
-            stage(invert, i, 1)
-            stage(multiply, i - 1)
-            stage(normalise, i)
-            stage(flip, i)
-            stage(group_x, i + 1)
+            for s in range(STREAMS):
+                stage(row_max, i + 1, s)
+            if i < B:
+                stage(finish, i - 2, 0)
+                stage(finish, i - 2, 1)
+                stage(finish, i - 2, 2)
+                invert(i, 0)
+                stage(finish, i - 2, 3)
+                stage(spread_x, i + 1)
+                invert(i, 1)
+                normalise(i, 0)
+                if (i, 1) != LAST:
+                    normalise(i, 1)
+                stage(group_p, i - 1)
+                if (i, 1) == LAST:
+                    normalise(i, 1)
+                flip(i, 0)
+                if (i, 1) != LAST:
+                    flip(i, 1)
+                for s in range(STREAMS):
+                    stage(quantise_p, i - 1, s)
+                stage(gather_x, i + 1)
+                stage(multiply, i - 1)
+                if (i, 1) == LAST:
+                    flip(i, 1)
+                stage(quantise_x, i)
+                if i >= 2:
+                    residual(nc.vector, i - 1, 2 if i - 1 <= GPSIMD_LAST else PACK)
+                stage(group_x, i + 1)
+            else:
+                group_p(B - 1)
+                quantise_p(B - 1, 0)
+                for j in range(PACK):
+                    if j == 2:
+                        quantise_p(B - 1, 1)
+                    finish(B - 2, j)
+                multiply(B - 1)
+                residual(nc.vector, B - 1, PACK)
+                for j in range(PACK):
+                    finish(B - 1, j)

@@ -18,12 +18,15 @@ STREAMS = 2
 C = 512
 N = 512
 ROW_TILES = C // P
-X_ROWS_ON_VECTOR = 56
-X_ROWS_ON_TENSOR = 48
-GPSIMD_FIRST, GPSIMD_LAST = 1, B - 4
-LAST = (B - 1, STREAMS - 1)
+RESID_COLUMNS, RESID_COLUMNS_ENDS = 64, 1024
 
 FLOPS = 2 * STREAMS * B * C * C * N
+
+
+def on_vector(b, s, j):
+    if b == 0:
+        return s == 0
+    return s == 0 and j >= 2
 
 
 def tile_interfusion_pb_t_kernel(tc, logits1, logits2, x1, x2, out):
@@ -37,19 +40,16 @@ def tile_interfusion_pb_t_kernel(tc, logits1, logits2, x1, x2, out):
         stat = ctx.enter_context(tc.tile_pool(name="stat", bufs=3 * STREAMS))
         work = ctx.enter_context(tc.tile_pool(name="work", bufs=2 * STREAMS))
         short = ctx.enter_context(tc.tile_pool(name="short", bufs=STREAMS))
-        single = ctx.enter_context(tc.tile_pool(name="single", bufs=1))
         flip_psum = ctx.enter_context(tc.psum_pool(name="flip_psum", bufs=4))
         acc_psum = ctx.enter_context(tc.psum_pool(name="acc_psum", bufs=4))
         ctx.enter_context(tc.manual_schedule())
 
         ident = const.tile([P, P], F32)
         make_identity(nc, ident[:])
-        ident_bf16 = const.tile([P, P], BF16)
-        make_identity(nc, ident_bf16[:])
 
         lg, xin, negmax, expd, rowsum, inv, prob, flipped = {}, {}, {}, {}, {}, {}, {}, {}
         p_grouped, p_codes, p_scales = {}, {}, {}
-        spread, x_grouped, x_codes, x_scales = {}, {}, {}, {}
+        x_grouped, x_codes, x_scales = {}, {}, {}
         resid, acc, result = {}, {}, {}
 
         def load_logits(b):
@@ -101,10 +101,10 @@ def tile_interfusion_pb_t_kernel(tc, logits1, logits2, x1, x2, out):
             prob[b, s] = work.tile([P, ROW_TILES, C], BF16, name="prob", tag="prob")
             for j in range(ROW_TILES):
                 p_row, exp_row, factor = prob[b, s][:, j, :], expd[b, s][:, j, :], inv[b, s][:, j : j + 1]
-                if (b, s) == LAST:
-                    nc.scalar.activation(out=p_row, in_=exp_row, func=ACT.Copy, scale=factor)
-                else:
+                if on_vector(b, s, j):
                     nc.vector.tensor_scalar_mul(out=p_row, in0=exp_row, scalar1=factor)
+                else:
+                    nc.scalar.activation(out=p_row, in_=exp_row, func=ACT.Copy, scale=factor)
 
         def flip(b, s):
             words = prob[b, s][:].bitcast(F32).rearrange("c j (q half) -> c j half q", half=2)
@@ -128,34 +128,12 @@ def tile_interfusion_pb_t_kernel(tc, logits1, logits2, x1, x2, out):
                         in_=flipped[b, s][pair][:].rearrange("q half c -> q c half"),
                     )
 
-        def spread_x(b):
-            for s in range(STREAMS):
-                spread[b, s] = acc_psum.tile([P, PACK, X_ROWS_ON_TENSOR, PACK], BF16, name="spread", tag="acc")
-                src = xin[b, s][:].rearrange("q t (m j) -> q j m t", j=PACK)[:, :, P - X_ROWS_ON_TENSOR :, :]
-                for j in range(0, PACK, 2):
-                    nc.tensor.matmul(
-                        spread[b, s][:, j : j + 2],
-                        lhsT=ident_bf16[:],
-                        rhs=src[:, j : j + 2],
-                        start=True,
-                        stop=True,
-                    )
-
-        def gather_x(b):
-            for s in range(STREAMS):
-                x_grouped[b, s] = work.tile([P, N, PACK], BF16, name="x_grouped", tag="x_grouped", align_bytes=64)
-                blocks = x_grouped[b, s][:].rearrange("q (j m) t -> q j m t", j=PACK)
-                nc.scalar.copy(out=blocks[:, :, P - X_ROWS_ON_TENSOR :, :], in_=spread[b, s][:])
-
-        def group_x(b):
-            cut = X_ROWS_ON_VECTOR if b < 2 else 0
-            for s in range(STREAMS):
-                dst = x_grouped[b, s][:].rearrange("q (j m) t -> q m t j", j=PACK)
-                src = xin[b, s][:].rearrange("q t (m j) -> q m t j", j=PACK)
-                if cut > 0:
-                    nc.vector.tensor_copy(out=dst[:, :cut], in_=src[:, :cut])
-                end = P - X_ROWS_ON_TENSOR
-                nc.scalar.copy(out=dst[:, cut:end], in_=src[:, cut:end])
+        def group_x(b, s):
+            x_grouped[b, s] = work.tile([P, N, PACK], BF16, name="x_grouped", tag="x_grouped", align_bytes=64)
+            nc.vector.tensor_copy(
+                out=x_grouped[b, s][:].rearrange("q (j m) t -> q m t j", j=PACK),
+                in_=xin[b, s][:].rearrange("q t (m j) -> q m t j", j=PACK),
+            )
 
         def quantise(grouped, codes, scales, label, b, s):
             codes[b, s] = work.tile([P, C], U32, name=label + "_codes", tag=label + "_codes", align_bytes=64)
@@ -173,19 +151,18 @@ def tile_interfusion_pb_t_kernel(tc, logits1, logits2, x1, x2, out):
         def quantise_p(b, s):
             quantise(p_grouped, p_codes, p_scales, "p", b, s)
 
-        def add_rows(engine, b, first, last):
+        def add_columns(engine, b, first, last):
             x_rows = [xin[b, s][:].rearrange("q t n -> q (t n)")[:, first:last] for s in range(STREAMS)]
             sums = resid[b][:].rearrange("m j c -> m (j c)")[:, first:last]
             engine.tensor_tensor(out=sums, in0=x_rows[0], in1=x_rows[1], op=ALU.add)
 
-        def residual(engine, b, blocks):
-            resid[b] = single.tile([P, PACK, C], F32, name="resid", tag="resid")
-            for j in range(blocks):
-                add_rows(engine, b, j * C, (j + 1) * C)
-
-        def residual_gpsimd(b):
-            add_rows(nc.gpsimd, b, 2 * C - 1, 3 * C)
-            add_rows(nc.gpsimd, b, 3 * C, 4 * C)
+        def residual(b):
+            resid[b] = short.tile([P, PACK, C], F32, name="resid", tag="resid")
+            cut = RESID_COLUMNS_ENDS if b in (0, B - 1) else RESID_COLUMNS
+            add_columns(nc.vector, b, 0, cut)
+            middle = (cut + PACK * C) // 2
+            add_columns(nc.gpsimd, b, cut - 1, middle)
+            add_columns(nc.gpsimd, b, middle, PACK * C)
 
         def multiply(b):
             acc[b] = []
@@ -217,60 +194,38 @@ def tile_interfusion_pb_t_kernel(tc, logits1, logits2, x1, x2, out):
         def stage(work_of, b, *more):
             if 0 <= b < B:
                 work_of(b, *more)
-
         for b in range(2):
             load_logits(b)
             load_x(b)
         for s in range(STREAMS):
             row_max(0, s)
-        for i in range(B + 1):
-            if GPSIMD_FIRST <= i - 2 <= GPSIMD_LAST:
-                residual_gpsimd(i - 2)
+        for i in range(B):
             stage(load_logits, i + 2)
             stage(load_x, i + 2)
-            stage(exponent, i)
+            exponent(i)
+            for s in range(STREAMS):
+                invert(i, s)
+                if i == 0:
+                    normalise(0, s)
+            if i > 0:
+                for s in range(STREAMS):
+                    normalise(i, s)
+            for s in range(STREAMS):
+                flip(i, s)
             if i == 0:
-                spread_x(0)
-                residual(nc.vector, 0, PACK)
-                gather_x(0)
-                group_x(0)
+                for s in range(STREAMS):
+                    group_x(0, s)
+            residual(i)
+            for j in range(PACK):
+                stage(finish, i - 1, j)
             for s in range(STREAMS):
                 stage(row_max, i + 1, s)
-            if i < B:
-                stage(finish, i - 2, 0)
-                stage(finish, i - 2, 1)
-                stage(finish, i - 2, 2)
-                invert(i, 0)
-                stage(finish, i - 2, 3)
-                stage(spread_x, i + 1)
-                invert(i, 1)
-                normalise(i, 0)
-                if (i, 1) != LAST:
-                    normalise(i, 1)
-                stage(group_p, i - 1)
-                if (i, 1) == LAST:
-                    normalise(i, 1)
-                flip(i, 0)
-                if (i, 1) != LAST:
-                    flip(i, 1)
-                for s in range(STREAMS):
-                    stage(quantise_p, i - 1, s)
-                stage(gather_x, i + 1)
-                stage(multiply, i - 1)
-                if (i, 1) == LAST:
-                    flip(i, 1)
-                stage(quantise_x, i)
-                if i >= 2:
-                    residual(nc.vector, i - 1, 2 if i - 1 <= GPSIMD_LAST else PACK)
-                stage(group_x, i + 1)
-            else:
-                group_p(B - 1)
-                quantise_p(B - 1, 0)
-                for j in range(PACK):
-                    if j == 2:
-                        quantise_p(B - 1, 1)
-                    finish(B - 2, j)
-                multiply(B - 1)
-                residual(nc.vector, B - 1, PACK)
-                for j in range(PACK):
-                    finish(B - 1, j)
+            group_p(i)
+            quantise_x(i)
+            for s in range(STREAMS):
+                quantise_p(i, s)
+            multiply(i)
+            for s in range(STREAMS):
+                stage(group_x, i + 1, s)
+        for j in range(PACK):
+            finish(B - 1, j)

@@ -80,9 +80,9 @@ def tile_interfusion_pb_t_kernel(tc, logits1, logits2, x1, x2, out):
                 )
 
         def exponent(b):
+            rowsum[b] = stat.tile([P, STREAMS, ROW_TILES], F32, name="rowsum", tag="rowsum")
             for s in range(STREAMS):
                 expd[b, s] = work.tile([P, ROW_TILES, C], F32, name="expd", tag="expd")
-                rowsum[b, s] = stat.tile([P, ROW_TILES], F32, name="rowsum", tag="rowsum")
                 for j in range(ROW_TILES):
                     nc.scalar.activation(
                         out=expd[b, s][:, j, :],
@@ -90,17 +90,17 @@ def tile_interfusion_pb_t_kernel(tc, logits1, logits2, x1, x2, out):
                         func=ACT.Exp,
                         bias=negmax[b, s][:, j : j + 1],
                         scale=1.0,
-                        accum_out=rowsum[b, s][:, j : j + 1],
+                        accum_out=rowsum[b][:, s, j : j + 1],
                     )
 
-        def invert(b, s):
-            inv[b, s] = stat.tile([P, ROW_TILES], F32, name="inv", tag="inv")
-            nc.vector.reciprocal(out=inv[b, s][:], in_=rowsum[b, s][:])
+        def invert(b):
+            inv[b] = stat.tile([P, STREAMS, ROW_TILES], F32, name="inv", tag="inv")
+            nc.vector.reciprocal(out=inv[b][:], in_=rowsum[b][:])
 
         def normalise(b, s):
             prob[b, s] = work.tile([P, ROW_TILES, C], BF16, name="prob", tag="prob")
             for j in range(ROW_TILES):
-                p_row, exp_row, factor = prob[b, s][:, j, :], expd[b, s][:, j, :], inv[b, s][:, j : j + 1]
+                p_row, exp_row, factor = prob[b, s][:, j, :], expd[b, s][:, j, :], inv[b][:, s, j : j + 1]
                 if on_vector(b, s, j):
                     nc.vector.tensor_scalar_mul(out=p_row, in0=exp_row, scalar1=factor)
                 else:
@@ -203,25 +203,21 @@ def tile_interfusion_pb_t_kernel(tc, logits1, logits2, x1, x2, out):
             stage(load_logits, i + 2)
             stage(load_x, i + 2)
             exponent(i)
-            for s in range(STREAMS):
-                invert(i, s)
-                if i == 0:
-                    normalise(0, s)
-            if i > 0:
-                for s in range(STREAMS):
-                    normalise(i, s)
-            for s in range(STREAMS):
-                flip(i, s)
             if i == 0:
                 for s in range(STREAMS):
                     group_x(0, s)
+            invert(i)
+            quantise_x(i)
+            for s in range(STREAMS):
+                normalise(i, s)
+            for s in range(STREAMS):
+                flip(i, s)
             residual(i)
             for j in range(PACK):
                 stage(finish, i - 1, j)
             for s in range(STREAMS):
                 stage(row_max, i + 1, s)
             group_p(i)
-            quantise_x(i)
             for s in range(STREAMS):
                 quantise_p(i, s)
             multiply(i)

from contextlib import ExitStack

import concourse.mybir as mybir
from concourse.masks import make_identity

F32 = mybir.dt.float32
BF16 = mybir.dt.bfloat16
U32 = mybir.dt.uint32
U8 = mybir.dt.uint8
FP8X4 = mybir.dt.float8_e4m3fn_x4
ALU = mybir.AluOpType
ACT = mybir.ActivationFunctionType

P = 128
PACK = 4
B = 8
STREAMS = 2
C = 512
N = 512
ROW_TILES = C // P
RESID_COLUMNS, RESID_COLUMNS_ENDS = 64, 1024

FLOPS = 2 * STREAMS * B * C * C * N


def on_vector(b, s, j):
    if b == 0:
        return s == 0
    return s == 0 and j >= 2


def tile_interfusion_pb_t_kernel(tc, logits1, logits2, x1, x2, out):
    nc = tc.nc
    logits = (logits1, logits2)
    xs = (x1, x2)

    with ExitStack() as ctx:
        const = ctx.enter_context(tc.tile_pool(name="const", bufs=1))
        in_pool = ctx.enter_context(tc.tile_pool(name="in_pool", bufs=4 * STREAMS))
        stat = ctx.enter_context(tc.tile_pool(name="stat", bufs=3 * STREAMS))
        work = ctx.enter_context(tc.tile_pool(name="work", bufs=2 * STREAMS))
        short = ctx.enter_context(tc.tile_pool(name="short", bufs=STREAMS))
        flip_psum = ctx.enter_context(tc.psum_pool(name="flip_psum", bufs=4))
        acc_psum = ctx.enter_context(tc.psum_pool(name="acc_psum", bufs=4))
        ctx.enter_context(tc.manual_schedule())

        ident = const.tile([P, P], F32)
        make_identity(nc, ident[:])

        lg, xin, negmax, expd, rowsum, inv, prob, flipped = {}, {}, {}, {}, {}, {}, {}, {}
        p_grouped, p_codes, p_scales = {}, {}, {}
        x_grouped, x_codes, x_scales = {}, {}, {}
        resid, acc, result = {}, {}, {}

        def load_logits(b):
            for s in range(STREAMS):
                lg[b, s] = in_pool.tile([P, ROW_TILES, C], BF16, name="lg", tag="lg")
                rows = logits[s][b].rearrange("(j p) k -> p j k", p=P)
                step = 1 if (b, s) == (0, 0) else ROW_TILES
                for j in range(0, ROW_TILES, step):
                    nc.sync.dma_start(out=lg[b, s][:, j : j + step, :], in_=rows[:, j : j + step, :])

        def load_x(b):
            for s in range(STREAMS):
                xin[b, s] = in_pool.tile([P, PACK, N], BF16, name="xin", tag="xin")
                nc.sync.dma_start(out=xin[b, s][:], in_=xs[s][b].rearrange("(q t) h w -> q t (h w)", t=PACK))

        def row_max(b, s):
            unused = short.tile([P, ROW_TILES, C], BF16, name="unused", tag="unused")
            negmax[b, s] = stat.tile([P, ROW_TILES], F32, name="negmax", tag="negmax")
            for j in range(ROW_TILES):
                nc.vector.tensor_scalar(
                    out=unused[:, j, :],
                    in0=lg[b, s][:, j, :],
                    scalar1=-1.0,
                    scalar2=None,
                    op0=ALU.mult,
                    op1=ALU.min,
                    accum_out=negmax[b, s][:, j : j + 1],
                )

        def exponent(b):
            rowsum[b] = stat.tile([P, STREAMS, ROW_TILES], F32, name="rowsum", tag="rowsum")
            for s in range(STREAMS):
                expd[b, s] = work.tile([P, ROW_TILES, C], F32, name="expd", tag="expd")
                for j in range(ROW_TILES):
                    nc.scalar.activation(
                        out=expd[b, s][:, j, :],
                        in_=lg[b, s][:, j, :],
                        func=ACT.Exp,
                        bias=negmax[b, s][:, j : j + 1],
                        scale=1.0,
                        accum_out=rowsum[b][:, s, j : j + 1],
                    )

        def invert(b):
            inv[b] = stat.tile([P, STREAMS, ROW_TILES], F32, name="inv", tag="inv")
            nc.vector.reciprocal(out=inv[b][:], in_=rowsum[b][:])

        def normalise(b, s):
            prob[b, s] = work.tile([P, ROW_TILES, C], BF16, name="prob", tag="prob")
            for j in range(ROW_TILES):
                p_row, exp_row, factor = prob[b, s][:, j, :], expd[b, s][:, j, :], inv[b][:, s, j : j + 1]
                if on_vector(b, s, j):
                    nc.vector.tensor_scalar_mul(out=p_row, in0=exp_row, scalar1=factor)
                else:
                    nc.scalar.activation(out=p_row, in_=exp_row, func=ACT.Copy, scale=factor)

        def flip(b, s):
            words = prob[b, s][:].bitcast(F32).rearrange("c j (q half) -> c j half q", half=2)
            flipped[b, s] = []
            for pair in range(ROW_TILES // 2):
                bank = flip_psum.tile([P, 2, 2 * P], F32, name="bank", tag="bank")
                for jj in range(2):
                    for half in range(2):
                        nc.tensor.transpose(
                            bank[:, half, jj * P : (jj + 1) * P], words[:, 2 * pair + jj, half, :], ident[:]
                        )
                flipped[b, s].append(bank)

        def group_p(b):
            for s in range(STREAMS):
                p_grouped[b, s] = short.tile([P, C, PACK], BF16, name="p_grouped", tag="p_grouped", align_bytes=64)
                as_words = p_grouped[b, s][:].bitcast(F32)
                for pair in range(ROW_TILES // 2):
                    nc.scalar.copy(
                        out=as_words[:, 2 * pair * P : 2 * (pair + 1) * P, :],
                        in_=flipped[b, s][pair][:].rearrange("q half c -> q c half"),
                    )

        def group_x(b, s):
            x_grouped[b, s] = work.tile([P, N, PACK], BF16, name="x_grouped", tag="x_grouped", align_bytes=64)
            nc.vector.tensor_copy(
                out=x_grouped[b, s][:].rearrange("q (j m) t -> q m t j", j=PACK),
                in_=xin[b, s][:].rearrange("q t (m j) -> q m t j", j=PACK),
            )

        def quantise(grouped, codes, scales, label, b, s):
            codes[b, s] = work.tile([P, C], U32, name=label + "_codes", tag=label + "_codes", align_bytes=64)
            scales[b, s] = work.tile([P, C], U8, name=label + "_scales", tag=label + "_scales", align_bytes=64)
            nc.vector.quantize_mx(
                out=codes[b, s][:].bitcast(FP8X4),
                scales=scales[b, s][:],
                in_=grouped[b, s][:].rearrange("q c t -> q (c t)"),
            )

        def quantise_x(b):
            for s in range(STREAMS):
                quantise(x_grouped, x_codes, x_scales, "x", b, s)

        def quantise_p(b, s):
            quantise(p_grouped, p_codes, p_scales, "p", b, s)

        def add_columns(engine, b, first, last):
            x_rows = [xin[b, s][:].rearrange("q t n -> q (t n)")[:, first:last] for s in range(STREAMS)]
            sums = resid[b][:].rearrange("m j c -> m (j c)")[:, first:last]
            engine.tensor_tensor(out=sums, in0=x_rows[0], in1=x_rows[1], op=ALU.add)

        def residual(b):
            resid[b] = short.tile([P, PACK, C], F32, name="resid", tag="resid")
            cut = RESID_COLUMNS_ENDS if b in (0, B - 1) else RESID_COLUMNS
            add_columns(nc.vector, b, 0, cut)
            middle = (cut + PACK * C) // 2
            add_columns(nc.gpsimd, b, cut - 1, middle)
            add_columns(nc.gpsimd, b, middle, PACK * C)

        def multiply(b):
            acc[b] = []
            for j in range(PACK):
                bank = acc_psum.tile([P, C], F32, name="acc", tag="acc")
                for s in range(STREAMS):
                    nc.tensor.matmul_mx(
                        out=bank[:],
                        lhsT=x_codes[b, s][:, j * P : (j + 1) * P].bitcast(FP8X4),
                        lhsT_scale=x_scales[b, s][:, j * P : (j + 1) * P],
                        rhs=p_codes[b, s][:].bitcast(FP8X4),
                        rhs_scale=p_scales[b, s][:],
                        start=(s == 0),
                        stop=(s == STREAMS - 1),
                    )
                acc[b].append(bank)

        def finish(b, j):
            if j % 2 == 0:
                result[b, j // 2] = work.tile([P, 2, C], F32, name="result", tag="result")
            pair = result[b, j // 2]
            nc.vector.tensor_tensor(out=pair[:, j % 2, :], in0=acc[b][j][:], in1=resid[b][:, j, :], op=ALU.add)
            rows = out[b].rearrange("(m j) h w -> m j (h w)", j=PACK)
            if b == B - 1:
                nc.sync.dma_start(out=rows[:, j : j + 1, :], in_=pair[:, j % 2 : j % 2 + 1, :])
            elif j % 2 == 1:
                nc.sync.dma_start(out=rows[:, j - 1 : j + 1, :], in_=pair[:])

        def stage(work_of, b, *more):
            if 0 <= b < B:
                work_of(b, *more)
        for b in range(2):
            load_logits(b)
            load_x(b)
        for s in range(STREAMS):
            row_max(0, s)
        for i in range(B):
            stage(load_logits, i + 2)
            stage(load_x, i + 2)
            exponent(i)
            if i == 0:
                for s in range(STREAMS):
                    group_x(0, s)
            invert(i)
            quantise_x(i)
            for s in range(STREAMS):
                normalise(i, s)
            for s in range(STREAMS):
                flip(i, s)
            residual(i)
            for j in range(PACK):
                stage(finish, i - 1, j)
            for s in range(STREAMS):
                stage(row_max, i + 1, s)
            group_p(i)
            for s in range(STREAMS):
                quantise_p(i, s)
            multiply(i)
            for s in range(STREAMS):
                stage(group_x, i + 1, s)
        for j in range(PACK):
            finish(B - 1, j)
